import numpy as np
import ml_dtypes


def mxq(x, axis, fmt="e4m3"):
    dtype, down = {"e4m3": (ml_dtypes.float8_e4m3fn, 7), "e5m2": (ml_dtypes.float8_e5m2, 14)}[fmt]
    v = np.moveaxis(np.asarray(x, np.float32).astype(ml_dtypes.bfloat16).astype(np.float64), axis, -1)
    blocks = v.reshape(v.shape[:-1] + (-1, 32))
    amax = np.abs(blocks).max(-1, keepdims=True)
    byte = np.maximum(np.where(amax > 0, np.frexp(amax)[1] - 1 + 127, 0) - down, 1)
    scale = np.exp2(byte - 127.0)
    codes = (blocks / scale).astype(np.float32).astype(dtype).astype(np.float64)
    return np.moveaxis((codes * scale).reshape(v.shape), -1, axis)


WIDE = False


def mx_kscale(k):
    if not WIDE:
        return np.ones(k)
    levels = np.array([10, -10, 5, -5, 0])
    if k % 512:
        return np.exp2(np.random.permutation(np.resize(levels, k // 32))).repeat(32)
    a = np.empty((k // 512, 16))
    for p in range(k // 512):
        a[p, :8] = np.random.permutation(np.resize(levels, 8))
        for g in range(8):
            far = levels[np.abs(levels - a[p, g]) >= 10]
            a[p, g + 8] = far[np.random.randint(len(far))]
    return np.exp2(a.ravel()).repeat(32)


BF16 = ml_dtypes.bfloat16


def bf(x):
    return np.asarray(x, np.float32).astype(BF16)


def f64(x):
    return np.asarray(x).astype(np.float64)


B, T, D, H, HK, HD, W = 2, 128, 8192, 8, 2, 128, 512
HALF = HD // 2
ROPE_BASE = 10000.0
EPS = 1e-6


def rope_cos_sin():
    inv_freq = 1.0 / ROPE_BASE ** (np.arange(0, HD, 2) / HD)
    freqs = np.arange(T)[:, None] * inv_freq[None, :]
    emb = np.concatenate([freqs, freqs], axis=-1)
    return np.cos(emb), np.sin(emb)


def rotate_half(u):
    return np.concatenate([-u[..., HALF:], u[..., :HALF]], axis=-1)


def heads(u, n):
    return u.reshape(B, T, n, HD).transpose(0, 2, 1, 3)


def l2_gain(u, gamma):
    return u / (np.sqrt((u * u).sum(-1, keepdims=True)) + EPS) * gamma


def setup_inputs():
    s = mx_kscale(D)
    return {"x": bf(np.random.standard_normal((B, T, D)) * s),
            "wq": bf(np.random.standard_normal((H * HD, D)) / np.sqrt(D) / s[None, :]),
            "wk": bf(np.random.standard_normal((HK * HD, D)) / np.sqrt(D) / s[None, :]),
            "wv": bf(np.random.standard_normal((HK * HD, D)) * 2.0 / np.sqrt(D) / s[None, :]),
            "gamma_q": bf(np.sqrt(HD) * (1.0 + 0.1 * np.random.standard_normal(HD))),
            "gamma_k": bf(np.sqrt(HD) * (1.0 + 0.1 * np.random.standard_normal(HD)))}


def reference(x, wq, wk, wv, gamma_q, gamma_k):
    xq = mxq(f64(x), 2, "e4m3")
    q = heads(xq @ mxq(f64(wq), 1, "e4m3").T, H)
    k = heads(xq @ mxq(f64(wk), 1, "e4m3").T, HK)
    v = heads(xq @ mxq(f64(wv), 1, "e4m3").T, HK)
    cos, sin = rope_cos_sin()
    q = q * cos + rotate_half(q) * sin
    k = k * cos + rotate_half(k) * sin
    q = l2_gain(q, f64(gamma_q))
    k = l2_gain(k, f64(gamma_k))
    return q, k, v

@@ -1,0 +1,332 @@
+import math
+from contextlib import ExitStack
+
+import concourse.mybir as mybir
+from concourse.masks import make_identity
+
+F32 = mybir.dt.float32
+BF16 = mybir.dt.bfloat16
+I32 = mybir.dt.int32
+U32 = mybir.dt.uint32
+U8 = mybir.dt.uint8
+FP8X4 = mybir.dt.float8_e4m3fn_x4
+ALU = mybir.AluOpType
+ACT = mybir.ActivationFunctionType
+
+P = 128
+PACK = 4
+K_PASS = P * PACK
+PASS_WORDS = K_PASS // 2
+BATCH = 2
+D_MODEL = 8192
+PASSES = D_MODEL // K_PASS
+HEAD = 128
+HALF = HEAD // 2
+PAIR = 2
+BANK = 512
+
+ROUND_UNITS = 8
+ROUND_BANKS = ROUND_UNITS // 2
+ROUND_CODES = ROUND_UNITS * P
+TILE_UNITS = 2 * ROUND_UNITS
+X_PASSES = ROUND_UNITS // BATCH
+X_TILES = PASSES // X_PASSES
+W_BUFS = 5
+FIRST_CUTS = 2
+
+ROPE_BASE = 10000.0
+EPS = 1e-6
+FREQ_STEP = ROPE_BASE ** (-1.0 / HALF)
+TWO_PI = 2.0 * math.pi
+TWO_PI_HIGH = 6.28125
+TWO_PI_LOW = TWO_PI - TWO_PI_HIGH
+ROUND_MAGIC = 1.5 * 2.0**23
+TINY = 1e-30
+
+FLOPS = 2 * BATCH * P * 12 * HEAD * D_MODEL
+
+
+def tile_gqaattention_pa_k_kernel(tc, x, wq, wk, wv, gamma_q, gamma_k, out_0, out_1, out_2):
+    nc = tc.nc
+    with ExitStack() as ctx:
+        ctx.enter_context(tc.manual_schedule())
+        const = ctx.enter_context(tc.tile_pool(name="const", bufs=1))
+        x_pool = ctx.enter_context(tc.tile_pool(name="x_raw", bufs=X_TILES))
+        w_pool = ctx.enter_context(tc.tile_pool(name="w_raw", bufs=W_BUFS))
+        grouped_pool = ctx.enter_context(tc.tile_pool(name="grouped", bufs=3))
+        codes_pool = ctx.enter_context(tc.tile_pool(name="codes", bufs=3))
+        u_pool = ctx.enter_context(tc.tile_pool(name="u", bufs=4))
+        rope_pool = ctx.enter_context(tc.tile_pool(name="rope", bufs=3))
+        bank_pool = ctx.enter_context(tc.psum_pool(name="banks", bufs=6))
+        acc_pool = ctx.enter_context(tc.psum_pool(name="acc", bufs=BATCH))
+
+        weights = [wq[0:BANK, :], wq[BANK : 2 * BANK, :], wk, wv]
+        w_order = []
+        for group in range(len(weights)):
+            blocks = weights[group].shape[0] // P
+            for t in range(PASSES * blocks // TILE_UNITS):
+                w_order.append((group, t))
+
+        def load_x(t, cuts):
+            x_raw = x_pool.tile([P, BATCH * X_PASSES * K_PASS], BF16)
+            width = X_PASSES * K_PASS // cuts
+            for cut in range(cuts):
+                first = t * X_PASSES * K_PASS + cut * width
+                nc.sync.dma_start(
+                    out=x_raw[:].rearrange("p (b k) -> p b k", b=BATCH)[:, :, cut * width : (cut + 1) * width],
+                    in_=x[:, :, first : first + width].rearrange("b t k -> t b k"),
+                )
+            return x_raw
+
+        def load_w(n, cuts):
+            group, t = w_order[n]
+            blocks = weights[group].shape[0] // P
+            tile_k = TILE_UNITS // blocks * K_PASS
+            w_raw = w_pool.tile([P, TILE_UNITS * K_PASS], BF16)
+            width = tile_k // cuts
+            for cut in range(cuts):
+                first = t * tile_k + cut * width
+                nc.sync.dma_start(
+                    out=w_raw[:].rearrange("p (j k) -> p j k", j=blocks)[:, :, cut * width : (cut + 1) * width],
+                    in_=weights[group][:, first : first + width].rearrange("(j p) k -> p j k", p=P),
+                )
+            return w_raw
+
+        gain_rows = const.tile([P, 2 * HEAD], BF16)
+        nc.vector.memset(gain_rows[:], 0.0)
+        nc.scalar.dma_start(out=gain_rows[0:1, 0:HEAD], in_=gamma_q.rearrange("(o d) -> o d", o=1))
+        nc.scalar.dma_start(out=gain_rows[0:1, HEAD : 2 * HEAD], in_=gamma_k.rearrange("(o d) -> o d", o=1))
+
+        x_tiles = []
+        w_tiles = []
+        for t in range(X_TILES):
+            x_tiles.append(load_x(t, FIRST_CUTS if t == 0 else 1))
+            w_tiles.append(load_w(t, FIRST_CUTS if t == 0 else 1))
+        for n in range(X_TILES, W_BUFS):
+            w_tiles.append(load_w(n, 1))
+
+        position_int = const.tile([P, 1], I32)
+        nc.gpsimd.iota(position_int[:], pattern=[[0, 1]], base=0, channel_multiplier=1)
+        identity = const.tile([P, P], F32)
+        make_identity(nc, identity[:])
+
+        ones = const.tile([P, P], BF16)
+        nc.vector.memset(ones[:], 1.0)
+        tiny = const.tile([P, 1], F32)
+        nc.vector.memset(tiny[:], TINY)
+
+        frequency = const.tile([P, HALF], F32)
+        nc.vector.memset(frequency[:, 0:1], 1.0)
+        for level in range(6):
+            width = 2**level
+            nc.vector.tensor_scalar_mul(
+                out=frequency[:, width : 2 * width], in0=frequency[:, 0:width], scalar1=FREQ_STEP**width
+            )
+        position = const.tile([P, 1], F32)
+        nc.vector.tensor_copy(out=position[:], in_=position_int[:])
+        angle = const.tile([P, 3 * HALF], F32)
+        nc.vector.tensor_scalar(
+            out=angle[:, 0:HALF], in0=frequency[:], scalar1=position[:, 0:1], scalar2=-1.0, op0=ALU.mult, op1=ALU.mult
+        )
+        nc.vector.tensor_scalar_mul(out=angle[:, HALF : 2 * HALF], in0=frequency[:], scalar1=position[:, 0:1])
+        nc.vector.tensor_scalar(
+            out=angle[:, 2 * HALF : 3 * HALF],
+            in0=frequency[:],
+            scalar1=position[:, 0:1],
+            scalar2=math.pi / 2.0,
+            op0=ALU.mult,
+            op1=ALU.add,
+        )
+        shifted = const.tile([P, 3 * HALF], F32)
+        nc.vector.tensor_scalar(
+            out=shifted[:], in0=angle[:], scalar1=1.0 / TWO_PI, scalar2=ROUND_MAGIC, op0=ALU.mult, op1=ALU.add
+        )
+        turns = const.tile([P, 3 * HALF], F32)
+        nc.vector.tensor_scalar_sub(out=turns[:], in0=shifted[:], scalar1=ROUND_MAGIC)
+        nearly = const.tile([P, 3 * HALF], F32)
+        nc.vector.scalar_tensor_tensor(
+            out=nearly[:], in0=turns[:], scalar=-TWO_PI_HIGH, in1=angle[:], op0=ALU.mult, op1=ALU.add
+        )
+        reduced = const.tile([P, 3 * HALF], F32)
+        nc.vector.scalar_tensor_tensor(
+            out=reduced[:], in0=turns[:], scalar=-TWO_PI_LOW, in1=nearly[:], op0=ALU.mult, op1=ALU.add
+        )
+        trig = const.tile([P, 3 * HALF], F32)
+        nc.scalar.activation(out=trig[:], in_=reduced[:], func=ACT.Sin)
+        warm = const.tile([P, 1], F32)
+        nc.scalar.activation(out=warm[:], in_=tiny[:], func=ACT.Sqrt)
+
+        cos_gain = const.tile([P, 2 * HEAD], F32)
+        sin_gain = const.tile([P, 2 * HEAD], F32)
+
+        def build_tables():
+            gain_bank = bank_pool.tile([P, BANK], F32, tag="bank")
+            nc.tensor.matmul(out=gain_bank[:, 0 : 2 * HEAD], lhsT=ones[:], rhs=gain_rows[:], start=True, stop=True)
+            nc.vector.tensor_tensor(
+                out=cos_gain[:].rearrange("p (s d) -> p s d", d=HALF),
+                in0=trig[:, 2 * HALF : 3 * HALF].unsqueeze(1).to_broadcast([P, 4, HALF]),
+                in1=gain_bank[:, 0 : 2 * HEAD].rearrange("p (s d) -> p s d", d=HALF),
+                op=ALU.mult,
+            )
+            nc.vector.tensor_tensor(
+                out=sin_gain[:].rearrange("p (w d) -> p w d", d=HEAD),
+                in0=trig[:, 0:HEAD].unsqueeze(1).to_broadcast([P, 2, HEAD]),
+                in1=gain_bank[:, 0 : 2 * HEAD].rearrange("p (w d) -> p w d", d=HEAD),
+                op=ALU.mult,
+            )
+
+        x_codes = const.tile([P, PASSES * BATCH * P], U32, align_bytes=64)
+        x_scales = const.tile([P, PASSES * BATCH * P], U8, align_bytes=64)
+
+        def transpose_and_regroup(raw, blocks, first_pass):
+            words = raw[:].bitcast(F32)
+            block_words = words.shape[1] // blocks
+            starts = [
+                j * block_words + (first_pass + r) * PASS_WORDS for r in range(ROUND_UNITS // blocks) for j in range(blocks)
+            ]
+            grouped = grouped_pool.tile([P, ROUND_CODES * PACK], BF16, align_bytes=64)
+            grouped_words = grouped[:].bitcast(F32)
+            for i in range(ROUND_BANKS):
+                bank = bank_pool.tile([P, BANK], F32, tag="bank")
+                for a in range(2):
+                    for u in range(2):
+                        start = starts[2 * i + a]
+                        nc.tensor.transpose(
+                            bank[:, (2 * a + u) * P : (2 * a + u + 1) * P],
+                            words[:, start + u : start + PASS_WORDS : 2],
+                            identity[:],
+                        )
+                copy = nc.vector.tensor_copy if i == 0 else nc.scalar.copy
+                copy(
+                    out=grouped_words[:, i * BANK : (i + 1) * BANK].rearrange("p (a r u) -> p a r u", a=2, u=2),
+                    in_=bank[:].rearrange("p (a u r) -> p a r u", a=2, u=2),
+                )
+            return grouped
+
+        def quantise(grouped, codes, scales):
+            part = ROUND_CODES // 2
+            for h in range(2):
+                nc.vector.quantize_mx(
+                    out=codes[:, h * part : (h + 1) * part].bitcast(FP8X4),
+                    scales=scales[:, h * part : (h + 1) * part],
+                    in_=grouped[:, h * part * PACK : (h + 1) * part * PACK],
+                )
+
+        def multiply(acc, blocks, first_pass, w_codes, w_scales):
+            features = blocks * P
+            for r in range(ROUND_UNITS // blocks):
+                c = first_pass + r
+                for b in range(BATCH):
+                    tokens = slice((c * BATCH + b) * P, (c * BATCH + b + 1) * P)
+                    nc.tensor.matmul_mx(
+                        out=acc[b][:],
+                        lhsT=x_codes[:, tokens].bitcast(FP8X4),
+                        lhsT_scale=x_scales[:, tokens],
+                        rhs=w_codes[:, r * features : (r + 1) * features].bitcast(FP8X4),
+                        rhs_scale=w_scales[:, r * features : (r + 1) * features],
+                        start=(c == 0),
+                        stop=(c == PASSES - 1),
+                    )
+
+        def rope_and_norm(u_pair, which, dest):
+            heads = u_pair.rearrange("p (h d) -> p h d", h=PAIR)
+            cos_table = cos_gain[:, which * HEAD : (which + 1) * HEAD]
+            sin_table = sin_gain[:, which * HEAD : (which + 1) * HEAD]
+            squares = rope_pool.tile([P, PAIR * HEAD], F32)
+            sum_squares = rope_pool.tile([P, PAIR], F32)
+            for h in range(PAIR):
+                nc.scalar.activation(
+                    out=squares[:, h * HEAD : (h + 1) * HEAD],
+                    in_=u_pair[:, h * HEAD : (h + 1) * HEAD],
+                    func=ACT.Square,
+                    accum_out=sum_squares[:, h : h + 1],
+                )
+            norm = rope_pool.tile([P, PAIR], F32)
+            nc.scalar.activation(out=norm[:], in_=sum_squares[:], func=ACT.Sqrt, bias=tiny[:, 0:1])
+            straight = rope_pool.tile([P, PAIR, HEAD], F32)
+            nc.vector.tensor_tensor(
+                out=straight[:], in0=heads, in1=cos_table.unsqueeze(1).to_broadcast([P, PAIR, HEAD]), op=ALU.mult
+            )
+            crossed = rope_pool.tile([P, PAIR, HEAD], F32)
+            nc.vector.tensor_tensor(
+                out=crossed[:, :, 0:HALF],
+                in0=heads[:, :, HALF:HEAD],
+                in1=sin_table[:, 0:HALF].unsqueeze(1).to_broadcast([P, PAIR, HALF]),
+                op=ALU.mult,
+            )
+            nc.vector.tensor_tensor(
+                out=crossed[:, :, HALF:HEAD],
+                in0=heads[:, :, 0:HALF],
+                in1=sin_table[:, HALF:HEAD].unsqueeze(1).to_broadcast([P, PAIR, HALF]),
+                op=ALU.mult,
+            )
+            norm_eps = rope_pool.tile([P, PAIR], F32)
+            nc.vector.tensor_scalar_add(out=norm_eps[:], in0=norm[:], scalar1=EPS)
+            rotated = rope_pool.tile([P, PAIR, HEAD], F32)
+            nc.vector.tensor_tensor(out=rotated[:], in0=straight[:], in1=crossed[:], op=ALU.add)
+            inverse = rope_pool.tile([P, PAIR], F32)
+            nc.vector.reciprocal(out=inverse[:], in_=norm_eps[:])
+            result = rope_pool.tile([P, PAIR, HEAD], F32)
+            nc.vector.tensor_tensor(
+                out=result[:], in0=rotated[:], in1=inverse[:].unsqueeze(2).to_broadcast([P, PAIR, HEAD]), op=ALU.mult
+            )
+            nc.sync.dma_start(out=dest.rearrange("h t d -> t h d"), in_=result[:])
+
+        rounds = []
+        for n in range(len(w_order)):
+            if n < X_TILES:
+                rounds.append(("x", n, 0))
+            for part in range(2):
+                rounds.append(("w", n, part))
+
+        made = {}
+        acc = []
+        rope_steps = []
+        ropes_done = 0
+        for i in range(len(rounds) + 1):
+            if i < len(rounds):
+                kind, n, part = rounds[i]
+                if kind == "x":
+                    grouped = transpose_and_regroup(x_tiles[n], BATCH, 0)
+                    span = slice(n * ROUND_CODES, (n + 1) * ROUND_CODES)
+                    quantise(grouped, x_codes[:, span], x_scales[:, span])
+                else:
+                    blocks = weights[w_order[n][0]].shape[0] // P
+                    grouped = transpose_and_regroup(w_tiles[n], blocks, part * (ROUND_UNITS // blocks))
+                    w_codes = codes_pool.tile([P, ROUND_CODES], U32, align_bytes=64)
+                    w_scales = codes_pool.tile([P, ROUND_CODES], U8, align_bytes=64)
+                    quantise(grouped, w_codes, w_scales)
+                    made[i] = (w_codes, w_scales)
+                    if part == 1 and n + W_BUFS < len(w_order):
+                        w_tiles.append(load_w(n + W_BUFS, 1))
+            if i > 0 and rounds[i - 1][0] == "w":
+                kind, n, part = rounds[i - 1]
+                group, t = w_order[n]
+                blocks = weights[group].shape[0] // P
+                first_pass = (2 * t + part) * (ROUND_UNITS // blocks)
+                if first_pass == 0:
+                    acc = [acc_pool.tile([P, blocks * P], F32, tag="acc", name="acc%d" % b) for b in range(BATCH)]
+                multiply(acc, blocks, first_pass, made[i - 1][0], made[i - 1][1])
+                if first_pass + ROUND_UNITS // blocks == PASSES:
+                    u_0 = u_pool.tile([P, blocks * P], F32, tag="u")
+                    nc.scalar.copy(out=u_0[:], in_=acc[0][:])
+                    u_1 = u_pool.tile([P, blocks * P], F32, tag="u")
+                    nc.vector.tensor_copy(out=u_1[:], in_=acc[1][:])
+                    if group == 0:
+                        build_tables()
+                    for pair in range(blocks // PAIR):
+                        for b, u in enumerate((u_0, u_1)):
+                            u_pair = u[:, pair * PAIR * HEAD : (pair + 1) * PAIR * HEAD]
+                            if group < 2:
+                                first_head = group * (BANK // HEAD) + pair * PAIR
+                                rope_steps.append((u_pair, 0, out_0[b, first_head : first_head + PAIR]))
+                            elif group == 2:
+                                rope_steps.append((u_pair, 1, out_1[b]))
+                            else:
+                                nc.sync.dma_start(
+                                    out=out_2[b].rearrange("h t d -> t h d"),
+                                    in_=u_pair.rearrange("p (h d) -> p h d", h=PAIR),
+                                )
+            if ropes_done < len(rope_steps):
+                rope_and_norm(*rope_steps[ropes_done])
+                ropes_done += 1

@@ -16,7 +16,7 @@ ACT = mybir.ActivationFunctionType
 P = 128
 PACK = 4
 K_PASS = P * PACK
-PASS_WORDS = K_PASS // 2
+RUN = 16
 BATCH = 2
 D_MODEL = 8192
 PASSES = D_MODEL // K_PASS
@@ -31,7 +31,7 @@ ROUND_CODES = ROUND_UNITS * P
 TILE_UNITS = 2 * ROUND_UNITS
 X_PASSES = ROUND_UNITS // BATCH
 X_TILES = PASSES // X_PASSES
-W_BUFS = 5
+W_BUFS = 4
 FIRST_CUTS = 2
 
 ROPE_BASE = 10000.0
@@ -53,6 +53,7 @@ def tile_gqaattention_pa_k_kernel(tc, x, wq, wk, wv, gamma_q, gamma_k, out_0, ou
         const = ctx.enter_context(tc.tile_pool(name="const", bufs=1))
         x_pool = ctx.enter_context(tc.tile_pool(name="x_raw", bufs=X_TILES))
         w_pool = ctx.enter_context(tc.tile_pool(name="w_raw", bufs=W_BUFS))
+        sorted_pool = ctx.enter_context(tc.tile_pool(name="sorted", bufs=3))
         grouped_pool = ctx.enter_context(tc.tile_pool(name="grouped", bufs=3))
         codes_pool = ctx.enter_context(tc.tile_pool(name="codes", bufs=3))
         u_pool = ctx.enter_context(tc.tile_pool(name="u", bufs=4))
@@ -178,26 +179,33 @@ def tile_gqaattention_pa_k_kernel(tc, x, wq, wk, wv, gamma_q, gamma_k, out_0, ou
         x_codes = const.tile([P, PASSES * BATCH * P], U32, align_bytes=64)
         x_scales = const.tile([P, PASSES * BATCH * P], U8, align_bytes=64)
 
-        def transpose_and_regroup(raw, blocks, first_pass):
-            words = raw[:].bitcast(F32)
-            block_words = words.shape[1] // blocks
-            starts = [
-                j * block_words + (first_pass + r) * PASS_WORDS for r in range(ROUND_UNITS // blocks) for j in range(blocks)
-            ]
+        def sort_halves(raw, blocks, first_pass):
+            span = ROUND_UNITS // blocks * K_PASS
+            source = raw[:].rearrange("p (j k) -> p j k", j=blocks)[:, :, first_pass * K_PASS : first_pass * K_PASS + span]
+            halves = sorted_pool.tile([P, ROUND_UNITS * K_PASS], BF16)
+            width = ROUND_UNITS * K_PASS // 2
+            for u in range(2):
+                nc.vector.tensor_copy(
+                    out=halves[:, u * width : (u + 1) * width].rearrange("p (j g i) -> p j g i", j=blocks, i=RUN),
+                    in_=source.rearrange("p j (g u i) -> p u j g i", u=2, i=RUN)[:, u],
+                )
+            return halves
+
+        def transpose_and_regroup(halves, blocks):
+            words = halves[:].bitcast(F32)
+            passes = ROUND_UNITS // blocks
+            units = [j * passes + r for r in range(passes) for j in range(blocks)]
             grouped = grouped_pool.tile([P, ROUND_CODES * PACK], BF16, align_bytes=64)
             grouped_words = grouped[:].bitcast(F32)
             for i in range(ROUND_BANKS):
                 bank = bank_pool.tile([P, BANK], F32, tag="bank")
                 for a in range(2):
                     for u in range(2):
-                        start = starts[2 * i + a]
+                        start = u * ROUND_CODES + units[2 * i + a] * P
                         nc.tensor.transpose(
-                            bank[:, (2 * a + u) * P : (2 * a + u + 1) * P],
-                            words[:, start + u : start + PASS_WORDS : 2],
-                            identity[:],
+                            bank[:, (2 * a + u) * P : (2 * a + u + 1) * P], words[:, start : start + P], identity[:]
                         )
-                copy = nc.vector.tensor_copy if i == 0 else nc.scalar.copy
-                copy(
+                nc.scalar.copy(
                     out=grouped_words[:, i * BANK : (i + 1) * BANK].rearrange("p (a r u) -> p a r u", a=2, u=2),
                     in_=bank[:].rearrange("p (a u r) -> p a r u", a=2, u=2),
                 )
@@ -279,34 +287,48 @@ def tile_gqaattention_pa_k_kernel(tc, x, wq, wk, wv, gamma_q, gamma_k, out_0, ou
             for part in range(2):
                 rounds.append(("w", n, part))
 
+        def blocks_of(i):
+            kind, n, part = rounds[i]
+            return BATCH if kind == "x" else weights[w_order[n][0]].shape[0] // P
+
+        sorted_halves = {}
+        grouped = {}
         made = {}
         acc = []
         rope_steps = []
         ropes_done = 0
-        for i in range(len(rounds) + 1):
+        for step in range(len(rounds) + 3):
+            i = step
             if i < len(rounds):
                 kind, n, part = rounds[i]
+                blocks = blocks_of(i)
+                raw = x_tiles[n] if kind == "x" else w_tiles[n]
+                sorted_halves[i] = sort_halves(raw, blocks, part * (ROUND_UNITS // blocks))
+                if kind == "w" and part == 1 and n + W_BUFS < len(w_order):
+                    w_tiles.append(load_w(n + W_BUFS, 1))
+            i = step - 1
+            if 0 <= i < len(rounds):
+                grouped[i] = transpose_and_regroup(sorted_halves[i], blocks_of(i))
+            i = step - 2
+            if 0 <= i < len(rounds):
+                kind, n, part = rounds[i]
                 if kind == "x":
-                    grouped = transpose_and_regroup(x_tiles[n], BATCH, 0)
                     span = slice(n * ROUND_CODES, (n + 1) * ROUND_CODES)
-                    quantise(grouped, x_codes[:, span], x_scales[:, span])
+                    quantise(grouped[i], x_codes[:, span], x_scales[:, span])
                 else:
-                    blocks = weights[w_order[n][0]].shape[0] // P
-                    grouped = transpose_and_regroup(w_tiles[n], blocks, part * (ROUND_UNITS // blocks))
                     w_codes = codes_pool.tile([P, ROUND_CODES], U32, align_bytes=64)
                     w_scales = codes_pool.tile([P, ROUND_CODES], U8, align_bytes=64)
-                    quantise(grouped, w_codes, w_scales)
+                    quantise(grouped[i], w_codes, w_scales)
                     made[i] = (w_codes, w_scales)
-                    if part == 1 and n + W_BUFS < len(w_order):
-                        w_tiles.append(load_w(n + W_BUFS, 1))
-            if i > 0 and rounds[i - 1][0] == "w":
-                kind, n, part = rounds[i - 1]
+            i = step - 3
+            if i >= 0 and rounds[i][0] == "w":
+                kind, n, part = rounds[i]
                 group, t = w_order[n]
-                blocks = weights[group].shape[0] // P
+                blocks = blocks_of(i)
                 first_pass = (2 * t + part) * (ROUND_UNITS // blocks)
                 if first_pass == 0:
                     acc = [acc_pool.tile([P, blocks * P], F32, tag="acc", name="acc%d" % b) for b in range(BATCH)]
-                multiply(acc, blocks, first_pass, made[i - 1][0], made[i - 1][1])
+                multiply(acc, blocks, first_pass, made[i][0], made[i][1])
                 if first_pass + ROUND_UNITS // blocks == PASSES:
                     u_0 = u_pool.tile([P, blocks * P], F32, tag="u")
                     nc.scalar.copy(out=u_0[:], in_=acc[0][:])

@@ -16,13 +16,14 @@ ACT = mybir.ActivationFunctionType
 P = 128
 PACK = 4
 K_PASS = P * PACK
+PASS_WORDS = K_PASS // 2
+UNSORTED_EVERY = 4
 RUN = 16
 BATCH = 2
 D_MODEL = 8192
 PASSES = D_MODEL // K_PASS
 HEAD = 128
 HALF = HEAD // 2
-PAIR = 2
 BANK = 512
 
 ROUND_UNITS = 8
@@ -57,7 +58,7 @@ def tile_gqaattention_pa_k_kernel(tc, x, wq, wk, wv, gamma_q, gamma_k, out_0, ou
         grouped_pool = ctx.enter_context(tc.tile_pool(name="grouped", bufs=3))
         codes_pool = ctx.enter_context(tc.tile_pool(name="codes", bufs=3))
         u_pool = ctx.enter_context(tc.tile_pool(name="u", bufs=4))
-        rope_pool = ctx.enter_context(tc.tile_pool(name="rope", bufs=3))
+        rope_pool = ctx.enter_context(tc.tile_pool(name="rope", bufs=2))
         bank_pool = ctx.enter_context(tc.psum_pool(name="banks", bufs=6))
         acc_pool = ctx.enter_context(tc.psum_pool(name="acc", bufs=BATCH))
 
@@ -179,11 +180,14 @@ def tile_gqaattention_pa_k_kernel(tc, x, wq, wk, wv, gamma_q, gamma_k, out_0, ou
         x_codes = const.tile([P, PASSES * BATCH * P], U32, align_bytes=64)
         x_scales = const.tile([P, PASSES * BATCH * P], U8, align_bytes=64)
 
+        def sorted_range(first_pass, passes):
+            return first_pass + (1 if first_pass % UNSORTED_EVERY == 0 else 0), first_pass + passes
+
         def sort_halves(raw, blocks, first_pass):
-            span = ROUND_UNITS // blocks * K_PASS
-            source = raw[:].rearrange("p (j k) -> p j k", j=blocks)[:, :, first_pass * K_PASS : first_pass * K_PASS + span]
+            begin, end = sorted_range(first_pass, ROUND_UNITS // blocks)
+            source = raw[:].rearrange("p (j k) -> p j k", j=blocks)[:, :, begin * K_PASS : end * K_PASS]
             halves = sorted_pool.tile([P, ROUND_UNITS * K_PASS], BF16)
-            width = ROUND_UNITS * K_PASS // 2
+            width = blocks * (end - begin) * K_PASS // 2
             for u in range(2):
                 nc.vector.tensor_copy(
                     out=halves[:, u * width : (u + 1) * width].rearrange("p (j g i) -> p j g i", j=blocks, i=RUN),
@@ -191,20 +195,27 @@ def tile_gqaattention_pa_k_kernel(tc, x, wq, wk, wv, gamma_q, gamma_k, out_0, ou
                 )
             return halves
 
-        def transpose_and_regroup(halves, blocks):
+        def transpose_and_regroup(raw, halves, blocks, first_pass):
+            raw_words = raw[:].bitcast(F32)
             words = halves[:].bitcast(F32)
-            passes = ROUND_UNITS // blocks
-            units = [j * passes + r for r in range(passes) for j in range(blocks)]
+            block_words = raw_words.shape[1] // blocks
+            begin, end = sorted_range(first_pass, ROUND_UNITS // blocks)
+            half_words = blocks * (end - begin) * P
+            units = [(j, first_pass + r) for r in range(ROUND_UNITS // blocks) for j in range(blocks)]
             grouped = grouped_pool.tile([P, ROUND_CODES * PACK], BF16, align_bytes=64)
             grouped_words = grouped[:].bitcast(F32)
             for i in range(ROUND_BANKS):
                 bank = bank_pool.tile([P, BANK], F32, tag="bank")
                 for a in range(2):
+                    j, c = units[2 * i + a]
                     for u in range(2):
-                        start = u * ROUND_CODES + units[2 * i + a] * P
-                        nc.tensor.transpose(
-                            bank[:, (2 * a + u) * P : (2 * a + u + 1) * P], words[:, start : start + P], identity[:]
-                        )
+                        if c < begin:
+                            start = j * block_words + c * PASS_WORDS
+                            source = raw_words[:, start + u : start + PASS_WORDS : 2]
+                        else:
+                            start = u * half_words + (j * (end - begin) + c - begin) * P
+                            source = words[:, start : start + P]
+                        nc.tensor.transpose(bank[:, (2 * a + u) * P : (2 * a + u + 1) * P], source, identity[:])
                 nc.scalar.copy(
                     out=grouped_words[:, i * BANK : (i + 1) * BANK].rearrange("p (a r u) -> p a r u", a=2, u=2),
                     in_=bank[:].rearrange("p (a u r) -> p a r u", a=2, u=2),
@@ -212,13 +223,7 @@ def tile_gqaattention_pa_k_kernel(tc, x, wq, wk, wv, gamma_q, gamma_k, out_0, ou
             return grouped
 
         def quantise(grouped, codes, scales):
-            part = ROUND_CODES // 2
-            for h in range(2):
-                nc.vector.quantize_mx(
-                    out=codes[:, h * part : (h + 1) * part].bitcast(FP8X4),
-                    scales=scales[:, h * part : (h + 1) * part],
-                    in_=grouped[:, h * part * PACK : (h + 1) * part * PACK],
-                )
+            nc.vector.quantize_mx(out=codes.bitcast(FP8X4), scales=scales, in_=grouped[:])
 
         def multiply(acc, blocks, first_pass, w_codes, w_scales):
             features = blocks * P
@@ -236,49 +241,76 @@ def tile_gqaattention_pa_k_kernel(tc, x, wq, wk, wv, gamma_q, gamma_k, out_0, ou
                         stop=(c == PASSES - 1),
                     )
 
-        def rope_and_norm(u_pair, which, dest):
-            heads = u_pair.rearrange("p (h d) -> p h d", h=PAIR)
+        def rope_pieces(u_tiles, which, dests):
+            heads = u_tiles[0].shape[1] // HEAD
             cos_table = cos_gain[:, which * HEAD : (which + 1) * HEAD]
             sin_table = sin_gain[:, which * HEAD : (which + 1) * HEAD]
-            squares = rope_pool.tile([P, PAIR * HEAD], F32)
-            sum_squares = rope_pool.tile([P, PAIR], F32)
-            for h in range(PAIR):
-                nc.scalar.activation(
-                    out=squares[:, h * HEAD : (h + 1) * HEAD],
-                    in_=u_pair[:, h * HEAD : (h + 1) * HEAD],
-                    func=ACT.Square,
-                    accum_out=sum_squares[:, h : h + 1],
+            views = [u[:].rearrange("p (h d) -> p h d", h=heads) for u in u_tiles]
+            sum_squares = rope_pool.tile([P, BATCH * heads], F32)
+            norm = rope_pool.tile([P, BATCH * heads], F32)
+            norm_eps = rope_pool.tile([P, BATCH * heads], F32)
+            inverse = rope_pool.tile([P, BATCH * heads], F32)
+            straight = [rope_pool.tile([P, heads, HEAD], F32, tag="straight", name="straight%d" % b) for b in range(BATCH)]
+            crossed = [rope_pool.tile([P, heads, HEAD], F32, tag="crossed", name="crossed%d" % b) for b in range(BATCH)]
+            rotated = [rope_pool.tile([P, heads, HEAD], F32, tag="rotated", name="rotated%d" % b) for b in range(BATCH)]
+
+            def multiply_straight(b):
+                nc.vector.tensor_tensor(
+                    out=straight[b][:],
+                    in0=views[b],
+                    in1=cos_table.unsqueeze(1).to_broadcast([P, heads, HEAD]),
+                    op=ALU.mult,
                 )
-            norm = rope_pool.tile([P, PAIR], F32)
-            nc.scalar.activation(out=norm[:], in_=sum_squares[:], func=ACT.Sqrt, bias=tiny[:, 0:1])
-            straight = rope_pool.tile([P, PAIR, HEAD], F32)
-            nc.vector.tensor_tensor(
-                out=straight[:], in0=heads, in1=cos_table.unsqueeze(1).to_broadcast([P, PAIR, HEAD]), op=ALU.mult
-            )
-            crossed = rope_pool.tile([P, PAIR, HEAD], F32)
-            nc.vector.tensor_tensor(
-                out=crossed[:, :, 0:HALF],
-                in0=heads[:, :, HALF:HEAD],
-                in1=sin_table[:, 0:HALF].unsqueeze(1).to_broadcast([P, PAIR, HALF]),
-                op=ALU.mult,
-            )
-            nc.vector.tensor_tensor(
-                out=crossed[:, :, HALF:HEAD],
-                in0=heads[:, :, 0:HALF],
-                in1=sin_table[:, HALF:HEAD].unsqueeze(1).to_broadcast([P, PAIR, HALF]),
-                op=ALU.mult,
-            )
-            norm_eps = rope_pool.tile([P, PAIR], F32)
-            nc.vector.tensor_scalar_add(out=norm_eps[:], in0=norm[:], scalar1=EPS)
-            rotated = rope_pool.tile([P, PAIR, HEAD], F32)
-            nc.vector.tensor_tensor(out=rotated[:], in0=straight[:], in1=crossed[:], op=ALU.add)
-            inverse = rope_pool.tile([P, PAIR], F32)
-            nc.vector.reciprocal(out=inverse[:], in_=norm_eps[:])
-            result = rope_pool.tile([P, PAIR, HEAD], F32)
-            nc.vector.tensor_tensor(
-                out=result[:], in0=rotated[:], in1=inverse[:].unsqueeze(2).to_broadcast([P, PAIR, HEAD]), op=ALU.mult
-            )
-            nc.sync.dma_start(out=dest.rearrange("h t d -> t h d"), in_=result[:])
+
+            def multiply_crossed(b):
+                for to, source in ((0, HALF), (HALF, 0)):
+                    nc.vector.tensor_tensor(
+                        out=crossed[b][:, :, to : to + HALF],
+                        in0=views[b][:, :, source : source + HALF],
+                        in1=sin_table[:, to : to + HALF].unsqueeze(1).to_broadcast([P, heads, HALF]),
+                        op=ALU.mult,
+                    )
+
+            def rotate(b):
+                nc.vector.tensor_tensor(out=rotated[b][:], in0=straight[b][:], in1=crossed[b][:], op=ALU.add)
+
+            def scale_and_store(b):
+                result = rope_pool.tile([P, heads, HEAD], F32)
+                for h in range(heads):
+                    nc.scalar.activation(
+                        out=result[:, h], in_=rotated[b][:, h], func=ACT.Copy, scale=inverse[:, b * heads + h : b * heads + h + 1]
+                    )
+                nc.sync.dma_start(out=dests[b].rearrange("h t d -> t h d"), in_=result[:])
+
+            def first():
+                for b in range(BATCH):
+                    for h in range(heads):
+                        squares = rope_pool.tile([P, HEAD], F32)
+                        nc.scalar.activation(
+                            out=squares[:],
+                            in_=views[b][:, h],
+                            func=ACT.Square,
+                            accum_out=sum_squares[:, b * heads + h : b * heads + h + 1],
+                        )
+                nc.scalar.activation(out=norm[:], in_=sum_squares[:], func=ACT.Sqrt, bias=tiny[:, 0:1])
+                multiply_straight(0)
+                multiply_crossed(0)
+
+            def second():
+                nc.vector.tensor_scalar_add(out=norm_eps[:], in0=norm[:], scalar1=EPS)
+                rotate(0)
+                nc.vector.reciprocal(out=inverse[:], in_=norm_eps[:])
+                multiply_straight(1)
+                scale_and_store(0)
+
+            def third():
+                multiply_crossed(1)
+
+            def fourth():
+                rotate(1)
+                scale_and_store(1)
+
+            return [first, second, third, fourth]
 
         rounds = []
         for n in range(len(w_order)):
@@ -291,24 +323,28 @@ def tile_gqaattention_pa_k_kernel(tc, x, wq, wk, wv, gamma_q, gamma_k, out_0, ou
             kind, n, part = rounds[i]
             return BATCH if kind == "x" else weights[w_order[n][0]].shape[0] // P
 
+        def raw_of(i):
+            kind, n, part = rounds[i]
+            blocks = blocks_of(i)
+            return x_tiles[n] if kind == "x" else w_tiles[n], blocks, part * (ROUND_UNITS // blocks)
+
         sorted_halves = {}
         grouped = {}
         made = {}
         acc = []
-        rope_steps = []
-        ropes_done = 0
+        pieces = []
+        pieces_done = 0
         for step in range(len(rounds) + 3):
             i = step
             if i < len(rounds):
-                kind, n, part = rounds[i]
-                blocks = blocks_of(i)
-                raw = x_tiles[n] if kind == "x" else w_tiles[n]
-                sorted_halves[i] = sort_halves(raw, blocks, part * (ROUND_UNITS // blocks))
-                if kind == "w" and part == 1 and n + W_BUFS < len(w_order):
-                    w_tiles.append(load_w(n + W_BUFS, 1))
+                sorted_halves[i] = sort_halves(*raw_of(i))
             i = step - 1
             if 0 <= i < len(rounds):
-                grouped[i] = transpose_and_regroup(sorted_halves[i], blocks_of(i))
+                kind, n, part = rounds[i]
+                raw, blocks, first_pass = raw_of(i)
+                grouped[i] = transpose_and_regroup(raw, sorted_halves[i], blocks, first_pass)
+                if kind == "w" and part == 1 and n + W_BUFS < len(w_order):
+                    w_tiles.append(load_w(n + W_BUFS, 1))
             i = step - 2
             if 0 <= i < len(rounds):
                 kind, n, part = rounds[i]
@@ -318,7 +354,7 @@ def tile_gqaattention_pa_k_kernel(tc, x, wq, wk, wv, gamma_q, gamma_k, out_0, ou
                 else:
                     w_codes = codes_pool.tile([P, ROUND_CODES], U32, align_bytes=64)
                     w_scales = codes_pool.tile([P, ROUND_CODES], U8, align_bytes=64)
-                    quantise(grouped[i], w_codes, w_scales)
+                    quantise(grouped[i], w_codes[:], w_scales[:])
                     made[i] = (w_codes, w_scales)
             i = step - 3
             if i >= 0 and rounds[i][0] == "w":
@@ -336,19 +372,16 @@ def tile_gqaattention_pa_k_kernel(tc, x, wq, wk, wv, gamma_q, gamma_k, out_0, ou
                     nc.vector.tensor_copy(out=u_1[:], in_=acc[1][:])
                     if group == 0:
                         build_tables()
-                    for pair in range(blocks // PAIR):
+                    if group < 2:
+                        first_head = group * (BANK // HEAD)
+                        pieces += rope_pieces((u_0, u_1), 0, [out_0[b, first_head : first_head + blocks] for b in range(BATCH)])
+                    elif group == 2:
+                        pieces += rope_pieces((u_0, u_1), 1, [out_1[b] for b in range(BATCH)])
+                    else:
                         for b, u in enumerate((u_0, u_1)):
-                            u_pair = u[:, pair * PAIR * HEAD : (pair + 1) * PAIR * HEAD]
-                            if group < 2:
-                                first_head = group * (BANK // HEAD) + pair * PAIR
-                                rope_steps.append((u_pair, 0, out_0[b, first_head : first_head + PAIR]))
-                            elif group == 2:
-                                rope_steps.append((u_pair, 1, out_1[b]))
-                            else:
-                                nc.sync.dma_start(
-                                    out=out_2[b].rearrange("h t d -> t h d"),
-                                    in_=u_pair.rearrange("p (h d) -> p h d", h=PAIR),
-                                )
-            if ropes_done < len(rope_steps):
-                rope_and_norm(*rope_steps[ropes_done])
-                ropes_done += 1
+                            nc.sync.dma_start(
+                                out=out_2[b].rearrange("h t d -> t h d"), in_=u[:].rearrange("p (h d) -> p h d", h=blocks)
+                            )
+            if pieces_done < len(pieces):
+                pieces[pieces_done]()
+                pieces_done += 1

@@ -16,9 +16,8 @@ ACT = mybir.ActivationFunctionType
 P = 128
 PACK = 4
 K_PASS = P * PACK
-PASS_WORDS = K_PASS // 2
-UNSORTED_EVERY = 4
-RUN = 16
+BLOCK = 32
+RUN = BLOCK // 2
 BATCH = 2
 D_MODEL = 8192
 PASSES = D_MODEL // K_PASS
@@ -26,13 +25,15 @@ HEAD = 128
 HALF = HEAD // 2
 BANK = 512
 
-ROUND_UNITS = 8
+ROWS = 2
+ROUND_PASSES = 4
+ROUND_UNITS = ROWS * ROUND_PASSES
 ROUND_BANKS = ROUND_UNITS // 2
 ROUND_CODES = ROUND_UNITS * P
-TILE_UNITS = 2 * ROUND_UNITS
-X_PASSES = ROUND_UNITS // BATCH
-X_TILES = PASSES // X_PASSES
-W_BUFS = 4
+ROUND_K = ROUND_PASSES * K_PASS
+PER_GROUP = PASSES // ROUND_PASSES
+W_BUFS = 8
+TABLE_STEP = 6
 FIRST_CUTS = 2
 
 ROPE_BASE = 10000.0
@@ -52,60 +53,52 @@ def tile_gqaattention_pa_k_kernel(tc, x, wq, wk, wv, gamma_q, gamma_k, out_0, ou
     with ExitStack() as ctx:
         ctx.enter_context(tc.manual_schedule())
         const = ctx.enter_context(tc.tile_pool(name="const", bufs=1))
-        x_pool = ctx.enter_context(tc.tile_pool(name="x_raw", bufs=X_TILES))
+        x_pool = ctx.enter_context(tc.tile_pool(name="x_raw", bufs=PER_GROUP))
         w_pool = ctx.enter_context(tc.tile_pool(name="w_raw", bufs=W_BUFS))
         sorted_pool = ctx.enter_context(tc.tile_pool(name="sorted", bufs=3))
-        grouped_pool = ctx.enter_context(tc.tile_pool(name="grouped", bufs=3))
-        codes_pool = ctx.enter_context(tc.tile_pool(name="codes", bufs=3))
-        u_pool = ctx.enter_context(tc.tile_pool(name="u", bufs=4))
+        grouped_pool = ctx.enter_context(tc.tile_pool(name="grouped", bufs=4))
+        codes_pool = ctx.enter_context(tc.tile_pool(name="codes", bufs=4))
         rope_pool = ctx.enter_context(tc.tile_pool(name="rope", bufs=2))
         bank_pool = ctx.enter_context(tc.psum_pool(name="banks", bufs=6))
         acc_pool = ctx.enter_context(tc.psum_pool(name="acc", bufs=BATCH))
 
-        weights = [wq[0:BANK, :], wq[BANK : 2 * BANK, :], wk, wv]
-        w_order = []
-        for group in range(len(weights)):
-            blocks = weights[group].shape[0] // P
-            for t in range(PASSES * blocks // TILE_UNITS):
-                w_order.append((group, t))
+        group_rows = ROWS * HEAD
+        groups = []
+        for g in range(wq.shape[0] // group_rows):
+            groups.append((wq[g * group_rows : (g + 1) * group_rows, :], 0, out_0[:, g * ROWS : (g + 1) * ROWS]))
+        groups.append((wk, 1, out_1))
+        groups.append((wv, None, out_2))
 
-        def load_x(t, cuts):
-            x_raw = x_pool.tile([P, BATCH * X_PASSES * K_PASS], BF16)
-            width = X_PASSES * K_PASS // cuts
+        def load(pool, source, t, cuts):
+            raw = pool.tile([P, ROWS * ROUND_K], BF16, tag="raw", name="raw")
+            width = ROUND_K // cuts
             for cut in range(cuts):
-                first = t * X_PASSES * K_PASS + cut * width
+                first = t * ROUND_K + cut * width
                 nc.sync.dma_start(
-                    out=x_raw[:].rearrange("p (b k) -> p b k", b=BATCH)[:, :, cut * width : (cut + 1) * width],
-                    in_=x[:, :, first : first + width].rearrange("b t k -> t b k"),
+                    out=raw[:].rearrange("p (j k) -> p j k", j=ROWS)[:, :, cut * width : (cut + 1) * width],
+                    in_=source[:, :, first : first + width],
                 )
-            return x_raw
+            return raw
 
-        def load_w(n, cuts):
-            group, t = w_order[n]
-            blocks = weights[group].shape[0] // P
-            tile_k = TILE_UNITS // blocks * K_PASS
-            w_raw = w_pool.tile([P, TILE_UNITS * K_PASS], BF16)
-            width = tile_k // cuts
-            for cut in range(cuts):
-                first = t * tile_k + cut * width
-                nc.sync.dma_start(
-                    out=w_raw[:].rearrange("p (j k) -> p j k", j=blocks)[:, :, cut * width : (cut + 1) * width],
-                    in_=weights[group][:, first : first + width].rearrange("(j p) k -> p j k", p=P),
-                )
-            return w_raw
+        def load_x(t):
+            return load(x_pool, x.rearrange("b t k -> t b k"), t, FIRST_CUTS if t == 0 else 1)
+
+        def load_w(n):
+            source = groups[n // PER_GROUP][0].rearrange("(j p) k -> p j k", p=P)
+            return load(w_pool, source, n % PER_GROUP, FIRST_CUTS if n == 0 else 1)
 
         gain_rows = const.tile([P, 2 * HEAD], BF16)
         nc.vector.memset(gain_rows[:], 0.0)
         nc.scalar.dma_start(out=gain_rows[0:1, 0:HEAD], in_=gamma_q.rearrange("(o d) -> o d", o=1))
         nc.scalar.dma_start(out=gain_rows[0:1, HEAD : 2 * HEAD], in_=gamma_k.rearrange("(o d) -> o d", o=1))
 
+        w_count = PER_GROUP * len(groups)
         x_tiles = []
         w_tiles = []
-        for t in range(X_TILES):
-            x_tiles.append(load_x(t, FIRST_CUTS if t == 0 else 1))
-            w_tiles.append(load_w(t, FIRST_CUTS if t == 0 else 1))
-        for n in range(X_TILES, W_BUFS):
-            w_tiles.append(load_w(n, 1))
+        for n in range(W_BUFS):
+            if n < PER_GROUP:
+                x_tiles.append(load_x(n))
+            w_tiles.append(load_w(n))
 
         position_int = const.tile([P, 1], I32)
         nc.gpsimd.iota(position_int[:], pattern=[[0, 1]], base=0, channel_multiplier=1)
@@ -180,42 +173,35 @@ def tile_gqaattention_pa_k_kernel(tc, x, wq, wk, wv, gamma_q, gamma_k, out_0, ou
         x_codes = const.tile([P, PASSES * BATCH * P], U32, align_bytes=64)
         x_scales = const.tile([P, PASSES * BATCH * P], U8, align_bytes=64)
 
-        def sorted_range(first_pass, passes):
-            return first_pass + (1 if first_pass % UNSORTED_EVERY == 0 else 0), first_pass + passes
-
-        def sort_halves(raw, blocks, first_pass):
-            begin, end = sorted_range(first_pass, ROUND_UNITS // blocks)
-            source = raw[:].rearrange("p (j k) -> p j k", j=blocks)[:, :, begin * K_PASS : end * K_PASS]
-            halves = sorted_pool.tile([P, ROUND_UNITS * K_PASS], BF16)
-            width = blocks * (end - begin) * K_PASS // 2
-            for u in range(2):
-                nc.vector.tensor_copy(
-                    out=halves[:, u * width : (u + 1) * width].rearrange("p (j g i) -> p j g i", j=blocks, i=RUN),
-                    in_=source.rearrange("p j (g u i) -> p u j g i", u=2, i=RUN)[:, u],
-                )
+        def sort_halves(raw, cuts):
+            halves = sorted_pool.tile([P, ROWS * ROUND_K], BF16)
+            width = ROUND_K // cuts
+            for cut in range(cuts):
+                span = slice(cut * width, (cut + 1) * width)
+                half_span = slice(cut * width // 2, (cut + 1) * width // 2)
+                source = raw[:].rearrange("p (j k) -> p j k", j=ROWS)[:, :, span]
+                for u in range(2):
+                    nc.vector.tensor_copy(
+                        out=halves[:]
+                        .rearrange("p (u j k) -> p u j k", u=2, j=ROWS)[:, u, :, half_span]
+                        .rearrange("p j (g i) -> p j g i", i=RUN),
+                        in_=source.rearrange("p j (g u i) -> p u j g i", u=2, i=RUN)[:, u],
+                    )
             return halves
 
-        def transpose_and_regroup(raw, halves, blocks, first_pass):
-            raw_words = raw[:].bitcast(F32)
+        def transpose_and_regroup(halves):
             words = halves[:].bitcast(F32)
-            block_words = raw_words.shape[1] // blocks
-            begin, end = sorted_range(first_pass, ROUND_UNITS // blocks)
-            half_words = blocks * (end - begin) * P
-            units = [(j, first_pass + r) for r in range(ROUND_UNITS // blocks) for j in range(blocks)]
+            units = [j * ROUND_PASSES + r for r in range(ROUND_PASSES) for j in range(ROWS)]
             grouped = grouped_pool.tile([P, ROUND_CODES * PACK], BF16, align_bytes=64)
             grouped_words = grouped[:].bitcast(F32)
             for i in range(ROUND_BANKS):
                 bank = bank_pool.tile([P, BANK], F32, tag="bank")
                 for a in range(2):
-                    j, c = units[2 * i + a]
                     for u in range(2):
-                        if c < begin:
-                            start = j * block_words + c * PASS_WORDS
-                            source = raw_words[:, start + u : start + PASS_WORDS : 2]
-                        else:
-                            start = u * half_words + (j * (end - begin) + c - begin) * P
-                            source = words[:, start : start + P]
-                        nc.tensor.transpose(bank[:, (2 * a + u) * P : (2 * a + u + 1) * P], source, identity[:])
+                        start = u * ROUND_CODES + units[2 * i + a] * P
+                        nc.tensor.transpose(
+                            bank[:, (2 * a + u) * P : (2 * a + u + 1) * P], words[:, start : start + P], identity[:]
+                        )
                 nc.scalar.copy(
                     out=grouped_words[:, i * BANK : (i + 1) * BANK].rearrange("p (a r u) -> p a r u", a=2, u=2),
                     in_=bank[:].rearrange("p (a u r) -> p a r u", a=2, u=2),
@@ -225,108 +211,78 @@ def tile_gqaattention_pa_k_kernel(tc, x, wq, wk, wv, gamma_q, gamma_k, out_0, ou
         def quantise(grouped, codes, scales):
             nc.vector.quantize_mx(out=codes.bitcast(FP8X4), scales=scales, in_=grouped[:])
 
-        def multiply(acc, blocks, first_pass, w_codes, w_scales):
-            features = blocks * P
-            for r in range(ROUND_UNITS // blocks):
-                c = first_pass + r
-                for b in range(BATCH):
+        def multiply(acc, first_pass, w_codes, w_scales):
+            for b in range(BATCH):
+                for r in range(ROUND_PASSES):
+                    c = first_pass + r
                     tokens = slice((c * BATCH + b) * P, (c * BATCH + b + 1) * P)
+                    features = slice(r * group_rows, (r + 1) * group_rows)
                     nc.tensor.matmul_mx(
                         out=acc[b][:],
                         lhsT=x_codes[:, tokens].bitcast(FP8X4),
                         lhsT_scale=x_scales[:, tokens],
-                        rhs=w_codes[:, r * features : (r + 1) * features].bitcast(FP8X4),
-                        rhs_scale=w_scales[:, r * features : (r + 1) * features],
+                        rhs=w_codes[:, features].bitcast(FP8X4),
+                        rhs_scale=w_scales[:, features],
                         start=(c == 0),
                         stop=(c == PASSES - 1),
                     )
 
-        def rope_pieces(u_tiles, which, dests):
-            heads = u_tiles[0].shape[1] // HEAD
+        def rope_pieces(u, which, dest):
+            heads = BATCH * ROWS
             cos_table = cos_gain[:, which * HEAD : (which + 1) * HEAD]
             sin_table = sin_gain[:, which * HEAD : (which + 1) * HEAD]
-            views = [u[:].rearrange("p (h d) -> p h d", h=heads) for u in u_tiles]
-            sum_squares = rope_pool.tile([P, BATCH * heads], F32)
-            norm = rope_pool.tile([P, BATCH * heads], F32)
-            norm_eps = rope_pool.tile([P, BATCH * heads], F32)
-            inverse = rope_pool.tile([P, BATCH * heads], F32)
-            straight = [rope_pool.tile([P, heads, HEAD], F32, tag="straight", name="straight%d" % b) for b in range(BATCH)]
-            crossed = [rope_pool.tile([P, heads, HEAD], F32, tag="crossed", name="crossed%d" % b) for b in range(BATCH)]
-            rotated = [rope_pool.tile([P, heads, HEAD], F32, tag="rotated", name="rotated%d" % b) for b in range(BATCH)]
+            view = u[:].rearrange("p (h d) -> p h d", h=heads)
+            sum_squares = rope_pool.tile([P, heads], F32)
+            norm = rope_pool.tile([P, heads], F32)
+            norm_eps = rope_pool.tile([P, heads], F32)
+            inverse = rope_pool.tile([P, heads], F32)
+            straight = rope_pool.tile([P, heads, HEAD], F32)
+            crossed = rope_pool.tile([P, heads, HEAD], F32)
+            rotated = rope_pool.tile([P, heads, HEAD], F32)
+            result = rope_pool.tile([P, heads, HEAD], F32)
 
-            def multiply_straight(b):
+            def first():
+                for h in range(heads):
+                    squares = rope_pool.tile([P, HEAD], F32)
+                    nc.scalar.activation(
+                        out=squares[:], in_=view[:, h], func=ACT.Square, accum_out=sum_squares[:, h : h + 1]
+                    )
+                nc.scalar.activation(out=norm[:], in_=sum_squares[:], func=ACT.Sqrt, bias=tiny[:, 0:1])
                 nc.vector.tensor_tensor(
-                    out=straight[b][:],
-                    in0=views[b],
-                    in1=cos_table.unsqueeze(1).to_broadcast([P, heads, HEAD]),
-                    op=ALU.mult,
+                    out=straight[:], in0=view, in1=cos_table.unsqueeze(1).to_broadcast([P, heads, HEAD]), op=ALU.mult
                 )
 
-            def multiply_crossed(b):
+            def second():
                 for to, source in ((0, HALF), (HALF, 0)):
                     nc.vector.tensor_tensor(
-                        out=crossed[b][:, :, to : to + HALF],
-                        in0=views[b][:, :, source : source + HALF],
+                        out=crossed[:, :, to : to + HALF],
+                        in0=view[:, :, source : source + HALF],
                         in1=sin_table[:, to : to + HALF].unsqueeze(1).to_broadcast([P, heads, HALF]),
                         op=ALU.mult,
                     )
 
-            def rotate(b):
-                nc.vector.tensor_tensor(out=rotated[b][:], in0=straight[b][:], in1=crossed[b][:], op=ALU.add)
-
-            def scale_and_store(b):
-                result = rope_pool.tile([P, heads, HEAD], F32)
-                for h in range(heads):
-                    nc.scalar.activation(
-                        out=result[:, h], in_=rotated[b][:, h], func=ACT.Copy, scale=inverse[:, b * heads + h : b * heads + h + 1]
-                    )
-                nc.sync.dma_start(out=dests[b].rearrange("h t d -> t h d"), in_=result[:])
-
-            def first():
-                for b in range(BATCH):
-                    for h in range(heads):
-                        squares = rope_pool.tile([P, HEAD], F32)
-                        nc.scalar.activation(
-                            out=squares[:],
-                            in_=views[b][:, h],
-                            func=ACT.Square,
-                            accum_out=sum_squares[:, b * heads + h : b * heads + h + 1],
-                        )
-                nc.scalar.activation(out=norm[:], in_=sum_squares[:], func=ACT.Sqrt, bias=tiny[:, 0:1])
-                multiply_straight(0)
-                multiply_crossed(0)
-
-            def second():
-                nc.vector.tensor_scalar_add(out=norm_eps[:], in0=norm[:], scalar1=EPS)
-                rotate(0)
-                nc.vector.reciprocal(out=inverse[:], in_=norm_eps[:])
-                multiply_straight(1)
-                scale_and_store(0)
-
             def third():
-                multiply_crossed(1)
+                nc.vector.tensor_scalar_add(out=norm_eps[:], in0=norm[:], scalar1=EPS)
+                nc.vector.tensor_tensor(out=rotated[:], in0=straight[:], in1=crossed[:], op=ALU.add)
+                nc.vector.reciprocal(out=inverse[:], in_=norm_eps[:])
 
             def fourth():
-                rotate(1)
-                scale_and_store(1)
+                for h in range(heads):
+                    nc.scalar.activation(
+                        out=result[:, h], in_=rotated[:, h], func=ACT.Copy, scale=inverse[:, h : h + 1]
+                    )
+                for b in range(BATCH):
+                    nc.sync.dma_start(
+                        out=dest[b].rearrange("h t d -> t h d"), in_=result[:, b * ROWS : (b + 1) * ROWS]
+                    )
 
             return [first, second, third, fourth]
 
         rounds = []
-        for n in range(len(w_order)):
-            if n < X_TILES:
-                rounds.append(("x", n, 0))
-            for part in range(2):
-                rounds.append(("w", n, part))
-
-        def blocks_of(i):
-            kind, n, part = rounds[i]
-            return BATCH if kind == "x" else weights[w_order[n][0]].shape[0] // P
-
-        def raw_of(i):
-            kind, n, part = rounds[i]
-            blocks = blocks_of(i)
-            return x_tiles[n] if kind == "x" else w_tiles[n], blocks, part * (ROUND_UNITS // blocks)
+        for n in range(w_count):
+            if n < PER_GROUP:
+                rounds.append(("x", n))
+            rounds.append(("w", n))
 
         sorted_halves = {}
         grouped = {}
@@ -334,20 +290,21 @@ def tile_gqaattention_pa_k_kernel(tc, x, wq, wk, wv, gamma_q, gamma_k, out_0, ou
         acc = []
         pieces = []
         pieces_done = 0
-        for step in range(len(rounds) + 3):
+        for step in range(len(rounds) + 4):
             i = step
             if i < len(rounds):
-                sorted_halves[i] = sort_halves(*raw_of(i))
+                kind, n = rounds[i]
+                sorted_halves[i] = sort_halves((x_tiles if kind == "x" else w_tiles)[n], FIRST_CUTS if n == 0 else 1)
+                if kind == "w" and n + W_BUFS < w_count:
+                    w_tiles.append(load_w(n + W_BUFS))
+            if step == TABLE_STEP:
+                build_tables()
             i = step - 1
             if 0 <= i < len(rounds):
-                kind, n, part = rounds[i]
-                raw, blocks, first_pass = raw_of(i)
-                grouped[i] = transpose_and_regroup(raw, sorted_halves[i], blocks, first_pass)
-                if kind == "w" and part == 1 and n + W_BUFS < len(w_order):
-                    w_tiles.append(load_w(n + W_BUFS, 1))
-            i = step - 2
+                grouped[i] = transpose_and_regroup(sorted_halves[i])
+            i = step - 3
             if 0 <= i < len(rounds):
-                kind, n, part = rounds[i]
+                kind, n = rounds[i]
                 if kind == "x":
                     span = slice(n * ROUND_CODES, (n + 1) * ROUND_CODES)
                     quantise(grouped[i], x_codes[:, span], x_scales[:, span])
@@ -356,32 +313,26 @@ def tile_gqaattention_pa_k_kernel(tc, x, wq, wk, wv, gamma_q, gamma_k, out_0, ou
                     w_scales = codes_pool.tile([P, ROUND_CODES], U8, align_bytes=64)
                     quantise(grouped[i], w_codes[:], w_scales[:])
                     made[i] = (w_codes, w_scales)
-            i = step - 3
-            if i >= 0 and rounds[i][0] == "w":
-                kind, n, part = rounds[i]
-                group, t = w_order[n]
-                blocks = blocks_of(i)
-                first_pass = (2 * t + part) * (ROUND_UNITS // blocks)
-                if first_pass == 0:
-                    acc = [acc_pool.tile([P, blocks * P], F32, tag="acc", name="acc%d" % b) for b in range(BATCH)]
-                multiply(acc, blocks, first_pass, made[i][0], made[i][1])
-                if first_pass + ROUND_UNITS // blocks == PASSES:
-                    u_0 = u_pool.tile([P, blocks * P], F32, tag="u")
-                    nc.scalar.copy(out=u_0[:], in_=acc[0][:])
-                    u_1 = u_pool.tile([P, blocks * P], F32, tag="u")
-                    nc.vector.tensor_copy(out=u_1[:], in_=acc[1][:])
-                    if group == 0:
-                        build_tables()
-                    if group < 2:
-                        first_head = group * (BANK // HEAD)
-                        pieces += rope_pieces((u_0, u_1), 0, [out_0[b, first_head : first_head + blocks] for b in range(BATCH)])
-                    elif group == 2:
-                        pieces += rope_pieces((u_0, u_1), 1, [out_1[b] for b in range(BATCH)])
-                    else:
-                        for b, u in enumerate((u_0, u_1)):
-                            nc.sync.dma_start(
-                                out=out_2[b].rearrange("h t d -> t h d"), in_=u[:].rearrange("p (h d) -> p h d", h=blocks)
-                            )
             if pieces_done < len(pieces):
                 pieces[pieces_done]()
                 pieces_done += 1
+            i = step - 4
+            if i >= 0 and rounds[i][0] == "w":
+                n = rounds[i][1]
+                group, t = divmod(n, PER_GROUP)
+                if t == 0:
+                    acc = [acc_pool.tile([P, group_rows], F32, tag="acc", name="acc%d" % b) for b in range(BATCH)]
+                multiply(acc, t * ROUND_PASSES, made[i][0], made[i][1])
+                if t == PER_GROUP - 1:
+                    which, dest = groups[group][1:]
+                    u = rope_pool.tile([P, BATCH * group_rows], F32)
+                    for b in range(BATCH):
+                        copy = nc.vector.tensor_copy if which is None and b == 1 else nc.scalar.copy
+                        copy(out=u[:, b * group_rows : (b + 1) * group_rows], in_=acc[b][:])
+                        if which is None:
+                            nc.sync.dma_start(
+                                out=dest[b].rearrange("h t d -> t h d"),
+                                in_=u[:, b * group_rows : (b + 1) * group_rows].rearrange("p (h d) -> p h d", h=ROWS),
+                            )
+                    if which is not None:
+                        pieces += rope_pieces(u, which, dest)

@@ -17,6 +17,7 @@ P = 128
 PACK = 4
 K_PASS = P * PACK
 BLOCK = 32
+UNSORTED_EVERY = 1
 RUN = BLOCK // 2
 BATCH = 2
 D_MODEL = 8192
@@ -173,38 +174,42 @@ def tile_gqaattention_pa_k_kernel(tc, x, wq, wk, wv, gamma_q, gamma_k, out_0, ou
         x_codes = const.tile([P, PASSES * BATCH * P], U32, align_bytes=64)
         x_scales = const.tile([P, PASSES * BATCH * P], U8, align_bytes=64)
 
-        def sort_halves(raw, cuts):
+        def unsorted_passes(t):
+            return 1 if t % UNSORTED_EVERY == 0 else 0
+
+        def sort_halves(raw, t, cuts):
             halves = sorted_pool.tile([P, ROWS * ROUND_K], BF16)
-            width = ROUND_K // cuts
             for cut in range(cuts):
-                span = slice(cut * width, (cut + 1) * width)
-                half_span = slice(cut * width // 2, (cut + 1) * width // 2)
-                source = raw[:].rearrange("p (j k) -> p j k", j=ROWS)[:, :, span]
+                begin = max(cut * ROUND_PASSES // cuts, unsorted_passes(t)) * K_PASS
+                end = (cut + 1) * ROUND_PASSES // cuts * K_PASS
+                source = raw[:].rearrange("p (j k) -> p j k", j=ROWS)[:, :, begin:end]
                 for u in range(2):
                     nc.vector.tensor_copy(
                         out=halves[:]
-                        .rearrange("p (u j k) -> p u j k", u=2, j=ROWS)[:, u, :, half_span]
+                        .rearrange("p (u j k) -> p u j k", u=2, j=ROWS)[:, u, :, begin // 2 : end // 2]
                         .rearrange("p j (g i) -> p j g i", i=RUN),
                         in_=source.rearrange("p j (g u i) -> p u j g i", u=2, i=RUN)[:, u],
                     )
             return halves
 
-        def transpose_and_regroup(halves):
+        def transpose_and_regroup(raw, halves, t):
+            raw_words = raw[:].bitcast(F32)
             words = halves[:].bitcast(F32)
-            units = [j * ROUND_PASSES + r for r in range(ROUND_PASSES) for j in range(ROWS)]
             grouped = grouped_pool.tile([P, ROUND_CODES * PACK], BF16, align_bytes=64)
             grouped_words = grouped[:].bitcast(F32)
-            for i in range(ROUND_BANKS):
+            for r in range(ROUND_BANKS):
                 bank = bank_pool.tile([P, BANK], F32, tag="bank")
-                for a in range(2):
+                for j in range(ROWS):
                     for u in range(2):
-                        start = u * ROUND_CODES + units[2 * i + a] * P
-                        nc.tensor.transpose(
-                            bank[:, (2 * a + u) * P : (2 * a + u + 1) * P], words[:, start : start + P], identity[:]
-                        )
+                        unit = j * ROUND_PASSES + r
+                        if r < unsorted_passes(t):
+                            source = raw_words[:, unit * 2 * P + u : (unit + 1) * 2 * P : 2]
+                        else:
+                            source = words[:, u * ROUND_CODES + unit * P : u * ROUND_CODES + (unit + 1) * P]
+                        nc.tensor.transpose(bank[:, (2 * j + u) * P : (2 * j + u + 1) * P], source, identity[:])
                 nc.scalar.copy(
-                    out=grouped_words[:, i * BANK : (i + 1) * BANK].rearrange("p (a r u) -> p a r u", a=2, u=2),
-                    in_=bank[:].rearrange("p (a u r) -> p a r u", a=2, u=2),
+                    out=grouped_words[:, r * BANK : (r + 1) * BANK].rearrange("p (j n u) -> p j n u", j=ROWS, u=2),
+                    in_=bank[:].rearrange("p (j u n) -> p j n u", j=ROWS, u=2),
                 )
             return grouped
 
@@ -284,6 +289,10 @@ def tile_gqaattention_pa_k_kernel(tc, x, wq, wk, wv, gamma_q, gamma_k, out_0, ou
                 rounds.append(("x", n))
             rounds.append(("w", n))
 
+        def raw_of(i):
+            kind, n = rounds[i]
+            return x_tiles[n] if kind == "x" else w_tiles[n]
+
         sorted_halves = {}
         grouped = {}
         made = {}
@@ -293,15 +302,16 @@ def tile_gqaattention_pa_k_kernel(tc, x, wq, wk, wv, gamma_q, gamma_k, out_0, ou
         for step in range(len(rounds) + 4):
             i = step
             if i < len(rounds):
-                kind, n = rounds[i]
-                sorted_halves[i] = sort_halves((x_tiles if kind == "x" else w_tiles)[n], FIRST_CUTS if n == 0 else 1)
-                if kind == "w" and n + W_BUFS < w_count:
-                    w_tiles.append(load_w(n + W_BUFS))
+                n = rounds[i][1]
+                sorted_halves[i] = sort_halves(raw_of(i), n % PER_GROUP, FIRST_CUTS if n == 0 else 1)
             if step == TABLE_STEP:
                 build_tables()
             i = step - 1
             if 0 <= i < len(rounds):
-                grouped[i] = transpose_and_regroup(sorted_halves[i])
+                kind, n = rounds[i]
+                grouped[i] = transpose_and_regroup(raw_of(i), sorted_halves[i], n % PER_GROUP)
+                if kind == "w" and n + W_BUFS < w_count:
+                    w_tiles.append(load_w(n + W_BUFS))
             i = step - 3
             if 0 <= i < len(rounds):
                 kind, n = rounds[i]

@@ -41,8 +41,6 @@ ROPE_BASE = 10000.0
 EPS = 1e-6
 FREQ_STEP = ROPE_BASE ** (-1.0 / HALF)
 TWO_PI = 2.0 * math.pi
-TWO_PI_HIGH = 6.28125
-TWO_PI_LOW = TWO_PI - TWO_PI_HIGH
 ROUND_MAGIC = 1.5 * 2.0**23
 TINY = 1e-30
 
@@ -106,49 +104,38 @@ def tile_gqaattention_pa_k_kernel(tc, x, wq, wk, wv, gamma_q, gamma_k, out_0, ou
         identity = const.tile([P, P], F32)
         make_identity(nc, identity[:])
 
+        fine = const.tile([P, 8], F32)
+        nc.vector.memset(fine[:, 0:1], 1.0)
+        coarse = const.tile([P, 8], F32)
+        nc.vector.tensor_scalar_mul(out=coarse[:, 0:1], in0=position_int[:], scalar1=1.0 / TWO_PI)
+        for width in (1, 2, 4):
+            for factors, step in ((fine, FREQ_STEP), (coarse, FREQ_STEP**8)):
+                nc.vector.tensor_scalar_mul(
+                    out=factors[:, width : 2 * width], in0=factors[:, 0:width], scalar1=step**width
+                )
+        phase = const.tile([P, 2 * HALF], F32)
+        nc.vector.tensor_tensor(
+            out=phase[:, 0:HALF].rearrange("p (m n) -> p m n", n=8),
+            in0=coarse[:].unsqueeze(2).to_broadcast([P, 8, 8]),
+            in1=fine[:].unsqueeze(1).to_broadcast([P, 8, 8]),
+            op=ALU.mult,
+        )
         ones = const.tile([P, P], BF16)
         nc.vector.memset(ones[:], 1.0)
+        nc.vector.tensor_scalar_add(out=phase[:, HALF : 2 * HALF], in0=phase[:, 0:HALF], scalar1=0.25)
         tiny = const.tile([P, 1], F32)
         nc.vector.memset(tiny[:], TINY)
-
-        frequency = const.tile([P, HALF], F32)
-        nc.vector.memset(frequency[:, 0:1], 1.0)
-        for level in range(6):
-            width = 2**level
-            nc.vector.tensor_scalar_mul(
-                out=frequency[:, width : 2 * width], in0=frequency[:, 0:width], scalar1=FREQ_STEP**width
-            )
-        position = const.tile([P, 1], F32)
-        nc.vector.tensor_copy(out=position[:], in_=position_int[:])
-        angle = const.tile([P, 3 * HALF], F32)
+        shifted = const.tile([P, 2 * HALF], F32)
         nc.vector.tensor_scalar(
-            out=angle[:, 0:HALF], in0=frequency[:], scalar1=position[:, 0:1], scalar2=-1.0, op0=ALU.mult, op1=ALU.mult
+            out=shifted[:], in0=phase[:], scalar1=1.0, scalar2=ROUND_MAGIC, op0=ALU.mult, op1=ALU.add
         )
-        nc.vector.tensor_scalar_mul(out=angle[:, HALF : 2 * HALF], in0=frequency[:], scalar1=position[:, 0:1])
-        nc.vector.tensor_scalar(
-            out=angle[:, 2 * HALF : 3 * HALF],
-            in0=frequency[:],
-            scalar1=position[:, 0:1],
-            scalar2=math.pi / 2.0,
-            op0=ALU.mult,
-            op1=ALU.add,
-        )
-        shifted = const.tile([P, 3 * HALF], F32)
-        nc.vector.tensor_scalar(
-            out=shifted[:], in0=angle[:], scalar1=1.0 / TWO_PI, scalar2=ROUND_MAGIC, op0=ALU.mult, op1=ALU.add
-        )
-        turns = const.tile([P, 3 * HALF], F32)
-        nc.vector.tensor_scalar_sub(out=turns[:], in0=shifted[:], scalar1=ROUND_MAGIC)
-        nearly = const.tile([P, 3 * HALF], F32)
+        missing = const.tile([P, 2 * HALF], F32)
         nc.vector.scalar_tensor_tensor(
-            out=nearly[:], in0=turns[:], scalar=-TWO_PI_HIGH, in1=angle[:], op0=ALU.mult, op1=ALU.add
-        )
-        reduced = const.tile([P, 3 * HALF], F32)
-        nc.vector.scalar_tensor_tensor(
-            out=reduced[:], in0=turns[:], scalar=-TWO_PI_LOW, in1=nearly[:], op0=ALU.mult, op1=ALU.add
+            out=missing[:], in0=shifted[:], scalar=ROUND_MAGIC, in1=phase[:], op0=ALU.subtract, op1=ALU.subtract
         )
         trig = const.tile([P, 3 * HALF], F32)
-        nc.scalar.activation(out=trig[:], in_=reduced[:], func=ACT.Sin)
+        nc.scalar.activation(out=trig[:, 0:HALF], in_=missing[:, 0:HALF], func=ACT.Sin, scale=TWO_PI)
+        nc.scalar.activation(out=trig[:, HALF : 3 * HALF], in_=missing[:], func=ACT.Sin, scale=-TWO_PI)
         warm = const.tile([P, 1], F32)
         nc.scalar.activation(out=warm[:], in_=tiny[:], func=ACT.Sqrt)
 
@@ -272,10 +259,12 @@ def tile_gqaattention_pa_k_kernel(tc, x, wq, wk, wv, gamma_q, gamma_k, out_0, ou
                 nc.vector.reciprocal(out=inverse[:], in_=norm_eps[:])
 
             def fourth():
-                for h in range(heads):
-                    nc.scalar.activation(
-                        out=result[:, h], in_=rotated[:, h], func=ACT.Copy, scale=inverse[:, h : h + 1]
-                    )
+                nc.vector.tensor_tensor(
+                    out=result[:],
+                    in0=rotated[:],
+                    in1=inverse[:].unsqueeze(2).to_broadcast([P, heads, HEAD]),
+                    op=ALU.mult,
+                )
                 for b in range(BATCH):
                     nc.sync.dma_start(
                         out=dest[b].rearrange("h t d -> t h d"), in_=result[:, b * ROWS : (b + 1) * ROWS]

import math
from contextlib import ExitStack

import concourse.mybir as mybir
from concourse.masks import make_identity

F32 = mybir.dt.float32
BF16 = mybir.dt.bfloat16
I32 = mybir.dt.int32
U32 = mybir.dt.uint32
U8 = mybir.dt.uint8
FP8X4 = mybir.dt.float8_e4m3fn_x4
ALU = mybir.AluOpType
ACT = mybir.ActivationFunctionType

P = 128
PACK = 4
K_PASS = P * PACK
BLOCK = 32
UNSORTED_EVERY = 1
RUN = BLOCK // 2
BATCH = 2
D_MODEL = 8192
PASSES = D_MODEL // K_PASS
HEAD = 128
HALF = HEAD // 2
BANK = 512

ROWS = 2
ROUND_PASSES = 4
ROUND_UNITS = ROWS * ROUND_PASSES
ROUND_BANKS = ROUND_UNITS // 2
ROUND_CODES = ROUND_UNITS * P
ROUND_K = ROUND_PASSES * K_PASS
PER_GROUP = PASSES // ROUND_PASSES
W_BUFS = 8
TABLE_STEP = 6
FIRST_CUTS = 2

ROPE_BASE = 10000.0
EPS = 1e-6
FREQ_STEP = ROPE_BASE ** (-1.0 / HALF)
TWO_PI = 2.0 * math.pi
ROUND_MAGIC = 1.5 * 2.0**23
TINY = 1e-30

FLOPS = 2 * BATCH * P * 12 * HEAD * D_MODEL


def tile_gqaattention_pa_k_kernel(tc, x, wq, wk, wv, gamma_q, gamma_k, out_0, out_1, out_2):
    nc = tc.nc
    with ExitStack() as ctx:
        ctx.enter_context(tc.manual_schedule())
        const = ctx.enter_context(tc.tile_pool(name="const", bufs=1))
        x_pool = ctx.enter_context(tc.tile_pool(name="x_raw", bufs=PER_GROUP))
        w_pool = ctx.enter_context(tc.tile_pool(name="w_raw", bufs=W_BUFS))
        sorted_pool = ctx.enter_context(tc.tile_pool(name="sorted", bufs=3))
        grouped_pool = ctx.enter_context(tc.tile_pool(name="grouped", bufs=4))
        codes_pool = ctx.enter_context(tc.tile_pool(name="codes", bufs=4))
        rope_pool = ctx.enter_context(tc.tile_pool(name="rope", bufs=2))
        bank_pool = ctx.enter_context(tc.psum_pool(name="banks", bufs=6))
        acc_pool = ctx.enter_context(tc.psum_pool(name="acc", bufs=BATCH))

        group_rows = ROWS * HEAD
        groups = []
        for g in range(wq.shape[0] // group_rows):
            groups.append((wq[g * group_rows : (g + 1) * group_rows, :], 0, out_0[:, g * ROWS : (g + 1) * ROWS]))
        groups.append((wk, 1, out_1))
        groups.append((wv, None, out_2))

        def load(pool, source, t, cuts):
            raw = pool.tile([P, ROWS * ROUND_K], BF16, tag="raw", name="raw")
            width = ROUND_K // cuts
            for cut in range(cuts):
                first = t * ROUND_K + cut * width
                nc.sync.dma_start(
                    out=raw[:].rearrange("p (j k) -> p j k", j=ROWS)[:, :, cut * width : (cut + 1) * width],
                    in_=source[:, :, first : first + width],
                )
            return raw

        def load_x(t):
            return load(x_pool, x.rearrange("b t k -> t b k"), t, FIRST_CUTS if t == 0 else 1)

        def load_w(n):
            source = groups[n // PER_GROUP][0].rearrange("(j p) k -> p j k", p=P)
            return load(w_pool, source, n % PER_GROUP, FIRST_CUTS if n == 0 else 1)

        gain_rows = const.tile([P, 2 * HEAD], BF16)
        nc.vector.memset(gain_rows[:], 0.0)
        nc.scalar.dma_start(out=gain_rows[0:1, 0:HEAD], in_=gamma_q.rearrange("(o d) -> o d", o=1))
        nc.scalar.dma_start(out=gain_rows[0:1, HEAD : 2 * HEAD], in_=gamma_k.rearrange("(o d) -> o d", o=1))

        w_count = PER_GROUP * len(groups)
        x_tiles = []
        w_tiles = []
        for n in range(W_BUFS):
            if n < PER_GROUP:
                x_tiles.append(load_x(n))
            w_tiles.append(load_w(n))

        position_int = const.tile([P, 1], I32)
        nc.gpsimd.iota(position_int[:], pattern=[[0, 1]], base=0, channel_multiplier=1)
        identity = const.tile([P, P], F32)
        make_identity(nc, identity[:])

        fine = const.tile([P, 8], F32)
        nc.vector.memset(fine[:, 0:1], 1.0)
        coarse = const.tile([P, 8], F32)
        nc.vector.tensor_scalar_mul(out=coarse[:, 0:1], in0=position_int[:], scalar1=1.0 / TWO_PI)
        for width in (1, 2, 4):
            for factors, step in ((fine, FREQ_STEP), (coarse, FREQ_STEP**8)):
                nc.vector.tensor_scalar_mul(
                    out=factors[:, width : 2 * width], in0=factors[:, 0:width], scalar1=step**width
                )
        phase = const.tile([P, 2 * HALF], F32)
        nc.vector.tensor_tensor(
            out=phase[:, 0:HALF].rearrange("p (m n) -> p m n", n=8),
            in0=coarse[:].unsqueeze(2).to_broadcast([P, 8, 8]),
            in1=fine[:].unsqueeze(1).to_broadcast([P, 8, 8]),
            op=ALU.mult,
        )
        ones = const.tile([P, P], BF16)
        nc.vector.memset(ones[:], 1.0)
        nc.vector.tensor_scalar_add(out=phase[:, HALF : 2 * HALF], in0=phase[:, 0:HALF], scalar1=0.25)
        tiny = const.tile([P, 1], F32)
        nc.vector.memset(tiny[:], TINY)
        shifted = const.tile([P, 2 * HALF], F32)
        nc.vector.tensor_scalar(
            out=shifted[:], in0=phase[:], scalar1=1.0, scalar2=ROUND_MAGIC, op0=ALU.mult, op1=ALU.add
        )
        missing = const.tile([P, 2 * HALF], F32)
        nc.vector.scalar_tensor_tensor(
            out=missing[:], in0=shifted[:], scalar=ROUND_MAGIC, in1=phase[:], op0=ALU.subtract, op1=ALU.subtract
        )
        trig = const.tile([P, 3 * HALF], F32)
        nc.scalar.activation(out=trig[:, 0:HALF], in_=missing[:, 0:HALF], func=ACT.Sin, scale=TWO_PI)
        nc.scalar.activation(out=trig[:, HALF : 3 * HALF], in_=missing[:], func=ACT.Sin, scale=-TWO_PI)
        warm = const.tile([P, 1], F32)
        nc.scalar.activation(out=warm[:], in_=tiny[:], func=ACT.Sqrt)

        cos_gain = const.tile([P, 2 * HEAD], F32)
        sin_gain = const.tile([P, 2 * HEAD], F32)

        def build_tables():
            gain_bank = bank_pool.tile([P, BANK], F32, tag="bank")
            nc.tensor.matmul(out=gain_bank[:, 0 : 2 * HEAD], lhsT=ones[:], rhs=gain_rows[:], start=True, stop=True)
            nc.vector.tensor_tensor(
                out=cos_gain[:].rearrange("p (s d) -> p s d", d=HALF),
                in0=trig[:, 2 * HALF : 3 * HALF].unsqueeze(1).to_broadcast([P, 4, HALF]),
                in1=gain_bank[:, 0 : 2 * HEAD].rearrange("p (s d) -> p s d", d=HALF),
                op=ALU.mult,
            )
            nc.vector.tensor_tensor(
                out=sin_gain[:].rearrange("p (w d) -> p w d", d=HEAD),
                in0=trig[:, 0:HEAD].unsqueeze(1).to_broadcast([P, 2, HEAD]),
                in1=gain_bank[:, 0 : 2 * HEAD].rearrange("p (w d) -> p w d", d=HEAD),
                op=ALU.mult,
            )

        x_codes = const.tile([P, PASSES * BATCH * P], U32, align_bytes=64)
        x_scales = const.tile([P, PASSES * BATCH * P], U8, align_bytes=64)

        def unsorted_passes(t):
            return 1 if t % UNSORTED_EVERY == 0 else 0

        def sort_halves(raw, t, cuts):
            halves = sorted_pool.tile([P, ROWS * ROUND_K], BF16)
            for cut in range(cuts):
                begin = max(cut * ROUND_PASSES // cuts, unsorted_passes(t)) * K_PASS
                end = (cut + 1) * ROUND_PASSES // cuts * K_PASS
                source = raw[:].rearrange("p (j k) -> p j k", j=ROWS)[:, :, begin:end]
                for u in range(2):
                    nc.vector.tensor_copy(
                        out=halves[:]
                        .rearrange("p (u j k) -> p u j k", u=2, j=ROWS)[:, u, :, begin // 2 : end // 2]
                        .rearrange("p j (g i) -> p j g i", i=RUN),
                        in_=source.rearrange("p j (g u i) -> p u j g i", u=2, i=RUN)[:, u],
                    )
            return halves

        def transpose_and_regroup(raw, halves, t):
            raw_words = raw[:].bitcast(F32)
            words = halves[:].bitcast(F32)
            grouped = grouped_pool.tile([P, ROUND_CODES * PACK], BF16, align_bytes=64)
            grouped_words = grouped[:].bitcast(F32)
            for r in range(ROUND_BANKS):
                bank = bank_pool.tile([P, BANK], F32, tag="bank")
                for j in range(ROWS):
                    for u in range(2):
                        unit = j * ROUND_PASSES + r
                        if r < unsorted_passes(t):
                            source = raw_words[:, unit * 2 * P + u : (unit + 1) * 2 * P : 2]
                        else:
                            source = words[:, u * ROUND_CODES + unit * P : u * ROUND_CODES + (unit + 1) * P]
                        nc.tensor.transpose(bank[:, (2 * j + u) * P : (2 * j + u + 1) * P], source, identity[:])
                nc.scalar.copy(
                    out=grouped_words[:, r * BANK : (r + 1) * BANK].rearrange("p (j n u) -> p j n u", j=ROWS, u=2),
                    in_=bank[:].rearrange("p (j u n) -> p j n u", j=ROWS, u=2),
                )
            return grouped

        def quantise(grouped, codes, scales):
            nc.vector.quantize_mx(out=codes.bitcast(FP8X4), scales=scales, in_=grouped[:])

        def multiply(acc, first_pass, w_codes, w_scales):
            for b in range(BATCH):
                for r in range(ROUND_PASSES):
                    c = first_pass + r
                    tokens = slice((c * BATCH + b) * P, (c * BATCH + b + 1) * P)
                    features = slice(r * group_rows, (r + 1) * group_rows)
                    nc.tensor.matmul_mx(
                        out=acc[b][:],
                        lhsT=x_codes[:, tokens].bitcast(FP8X4),
                        lhsT_scale=x_scales[:, tokens],
                        rhs=w_codes[:, features].bitcast(FP8X4),
                        rhs_scale=w_scales[:, features],
                        start=(c == 0),
                        stop=(c == PASSES - 1),
                    )

        def rope_pieces(u, which, dest):
            heads = BATCH * ROWS
            cos_table = cos_gain[:, which * HEAD : (which + 1) * HEAD]
            sin_table = sin_gain[:, which * HEAD : (which + 1) * HEAD]
            view = u[:].rearrange("p (h d) -> p h d", h=heads)
            sum_squares = rope_pool.tile([P, heads], F32)
            norm = rope_pool.tile([P, heads], F32)
            norm_eps = rope_pool.tile([P, heads], F32)
            inverse = rope_pool.tile([P, heads], F32)
            straight = rope_pool.tile([P, heads, HEAD], F32)
            crossed = rope_pool.tile([P, heads, HEAD], F32)
            rotated = rope_pool.tile([P, heads, HEAD], F32)
            result = rope_pool.tile([P, heads, HEAD], F32)

            def first():
                for h in range(heads):
                    squares = rope_pool.tile([P, HEAD], F32)
                    nc.scalar.activation(
                        out=squares[:], in_=view[:, h], func=ACT.Square, accum_out=sum_squares[:, h : h + 1]
                    )
                nc.scalar.activation(out=norm[:], in_=sum_squares[:], func=ACT.Sqrt, bias=tiny[:, 0:1])
                nc.vector.tensor_tensor(
                    out=straight[:], in0=view, in1=cos_table.unsqueeze(1).to_broadcast([P, heads, HEAD]), op=ALU.mult
                )

            def second():
                for to, source in ((0, HALF), (HALF, 0)):
                    nc.vector.tensor_tensor(
                        out=crossed[:, :, to : to + HALF],
                        in0=view[:, :, source : source + HALF],
                        in1=sin_table[:, to : to + HALF].unsqueeze(1).to_broadcast([P, heads, HALF]),
                        op=ALU.mult,
                    )

            def third():
                nc.vector.tensor_scalar_add(out=norm_eps[:], in0=norm[:], scalar1=EPS)
                nc.vector.tensor_tensor(out=rotated[:], in0=straight[:], in1=crossed[:], op=ALU.add)
                nc.vector.reciprocal(out=inverse[:], in_=norm_eps[:])

            def fourth():
                nc.vector.tensor_tensor(
                    out=result[:],
                    in0=rotated[:],
                    in1=inverse[:].unsqueeze(2).to_broadcast([P, heads, HEAD]),
                    op=ALU.mult,
                )
                for b in range(BATCH):
                    nc.sync.dma_start(
                        out=dest[b].rearrange("h t d -> t h d"), in_=result[:, b * ROWS : (b + 1) * ROWS]
                    )

            return [first, second, third, fourth]

        rounds = []
        for n in range(w_count):
            if n < PER_GROUP:
                rounds.append(("x", n))
            rounds.append(("w", n))

        def raw_of(i):
            kind, n = rounds[i]
            return x_tiles[n] if kind == "x" else w_tiles[n]

        sorted_halves = {}
        grouped = {}
        made = {}
        acc = []
        pieces = []
        pieces_done = 0
        for step in range(len(rounds) + 4):
            i = step
            if i < len(rounds):
                n = rounds[i][1]
                sorted_halves[i] = sort_halves(raw_of(i), n % PER_GROUP, FIRST_CUTS if n == 0 else 1)
            if step == TABLE_STEP:
                build_tables()
            i = step - 1
            if 0 <= i < len(rounds):
                kind, n = rounds[i]
                grouped[i] = transpose_and_regroup(raw_of(i), sorted_halves[i], n % PER_GROUP)
                if kind == "w" and n + W_BUFS < w_count:
                    w_tiles.append(load_w(n + W_BUFS))
            i = step - 3
            if 0 <= i < len(rounds):
                kind, n = rounds[i]
                if kind == "x":
                    span = slice(n * ROUND_CODES, (n + 1) * ROUND_CODES)
                    quantise(grouped[i], x_codes[:, span], x_scales[:, span])
                else:
                    w_codes = codes_pool.tile([P, ROUND_CODES], U32, align_bytes=64)
                    w_scales = codes_pool.tile([P, ROUND_CODES], U8, align_bytes=64)
                    quantise(grouped[i], w_codes[:], w_scales[:])
                    made[i] = (w_codes, w_scales)
            if pieces_done < len(pieces):
                pieces[pieces_done]()
                pieces_done += 1
            i = step - 4
            if i >= 0 and rounds[i][0] == "w":
                n = rounds[i][1]
                group, t = divmod(n, PER_GROUP)
                if t == 0:
                    acc = [acc_pool.tile([P, group_rows], F32, tag="acc", name="acc%d" % b) for b in range(BATCH)]
                multiply(acc, t * ROUND_PASSES, made[i][0], made[i][1])
                if t == PER_GROUP - 1:
                    which, dest = groups[group][1:]
                    u = rope_pool.tile([P, BATCH * group_rows], F32)
                    for b in range(BATCH):
                        copy = nc.vector.tensor_copy if which is None and b == 1 else nc.scalar.copy
                        copy(out=u[:, b * group_rows : (b + 1) * group_rows], in_=acc[b][:])
                        if which is None:
                            nc.sync.dma_start(
                                out=dest[b].rearrange("h t d -> t h d"),
                                in_=u[:, b * group_rows : (b + 1) * group_rows].rearrange("p (h d) -> p h d", h=ROWS),
                            )
                    if which is not None:
                        pieces += rope_pieces(u, which, dest)
